import numpy as np
import ml_dtypes


def mxq(x, axis, fmt="e4m3"):
    dtype, down = {"e4m3": (ml_dtypes.float8_e4m3fn, 7), "e5m2": (ml_dtypes.float8_e5m2, 14)}[fmt]
    v = np.moveaxis(np.asarray(x, np.float32).astype(ml_dtypes.bfloat16).astype(np.float64), axis, -1)
    blocks = v.reshape(v.shape[:-1] + (-1, 32))
    amax = np.abs(blocks).max(-1, keepdims=True)
    byte = np.maximum(np.where(amax > 0, np.frexp(amax)[1] - 1 + 127, 0) - down, 1)
    scale = np.exp2(byte - 127.0)
    codes = (blocks / scale).astype(np.float32).astype(dtype).astype(np.float64)
    return np.moveaxis((codes * scale).reshape(v.shape), -1, axis)


WIDE = False


def mx_kscale(k):
    if not WIDE:
        return np.ones(k)
    levels = np.array([10, -10, 5, -5, 0])
    a = np.random.permutation(np.resize(levels, k // 512 * 4)).reshape(k // 512, 4)
    idx = np.arange(k)
    return np.exp2(a[idx // 512, idx % 128 // 32])


BF16 = ml_dtypes.bfloat16


def bf(x):
    return np.asarray(x, np.float32).astype(BF16)


def f64(x):
    return np.asarray(x).astype(np.float64)


E2M1 = np.array([0.0, 0.5, 1.0, 1.5, 2.0, 3.0, 4.0, 6.0, -0.0, -0.5, -1.0, -1.5, -2.0, -3.0, -4.0, -6.0])


def pack_weight(w, fmt):
    k, n = w.shape
    w = f64(bf(w)).reshape(k // 32, 32, n)
    amax = np.abs(w).max(1)
    if fmt == "e4m3":
        byte = np.frexp(amax)[1] - 1 + 127 - 7
    else:
        mant, ex = np.frexp(amax / 6.0)
        byte = np.where(mant > 0.5, ex, ex - 1) + 127
    byte = np.clip(np.where(amax > 0, byte, 1), 1, 254)
    scaled = (w * np.exp2(127.0 - byte)[:, None, :]).reshape(k, n).astype(np.float32)
    by_word = np.ascontiguousarray(scaled.reshape(k // 512, 128, 4, n).transpose(0, 1, 3, 2))
    if fmt == "e4m3":
        words = by_word.astype(ml_dtypes.float8_e4m3fn).view(np.uint8)
    else:
        c = by_word.astype(ml_dtypes.float4_e2m1fn).view(np.uint8) & 0xF
        words = c[..., 0::2] | (c[..., 1::2] << 4)
    return np.ascontiguousarray(words), np.ascontiguousarray(byte.astype(np.uint8).reshape(k // 512, 16, n))


def unpack_weight(words, scales, fmt):
    g, p, n, _ = words.shape
    if fmt == "e4m3":
        vals = np.ascontiguousarray(words).view(ml_dtypes.float8_e4m3fn).astype(np.float64)
    else:
        nib = np.empty((g, p, n, 4), np.uint8)
        nib[..., 0::2] = words & 0xF
        nib[..., 1::2] = words >> 4
        vals = E2M1[nib]
    vals = vals * np.repeat(np.exp2(scales.astype(np.float64) - 127.0), 8, axis=1)[..., None]
    return vals.transpose(0, 1, 3, 2).reshape(g * 512, n)


B, C, W, H, K, S, NEW = 1, 124, 32, 32, 8, 2, 1
KK = K * K
IN = 2 * K * C + KK
OUT = C * NEW * NEW * KK
BN_EPS = 1e-5
FMT = "e4m3"


def unfold(x, oh, ow):
    p = (K - 1) // 2
    xp = np.pad(x, ((0, 0), (0, 0), (p, p), (p, p)))
    rows = []
    for i in range(K):
        cols = []
        for j in range(K):
            cols.append(xp[:, :, i:i + S * (oh - 1) + 1:S, j:j + S * (ow - 1) + 1:S])
        rows.append(np.stack(cols, axis=2))
    return np.stack(rows, axis=2)


def setup_inputs():
    s = mx_kscale(IN)
    sc = s[KK:KK + C * K:K]
    col = np.concatenate([np.full(KK, sc.max()), np.repeat(sc, K), np.repeat(sc, K)])
    so = np.repeat(sc, KK * NEW * NEW)
    x = bf(np.random.standard_normal((B, C, W, H)) * sc[None, :, None, None])
    conv_w = np.random.standard_normal((OUT, IN)) * 0.16 / np.sqrt(IN) / col
    words, scales = pack_weight(np.ascontiguousarray(conv_w.T), FMT)
    return {"x": x,
            "conv_w_words": words,
            "conv_w_scales": scales,
            "bn_gamma": bf((0.2 + 0.02 * np.random.standard_normal(OUT)) / so),
            "bn_beta": bf(0.4 * np.random.standard_normal(OUT) / so),
            "bn_mean": bf(0.1 * np.random.standard_normal(OUT)),
            "bn_var": bf(BN_EPS * (15.0 + 25.0 * np.random.random(OUT)))}


def reference(x, conv_w_words, conv_w_scales, bn_gamma, bn_beta, bn_mean, bn_var):
    x = f64(x)
    oh = -(-W // S)
    ow = -(-H // S)
    patches = unfold(x, oh, ow)
    x1 = patches.max(axis=1).reshape(B, KK, oh, ow)
    x2 = patches.max(axis=2).reshape(B, C * K, oh, ow)
    x3 = patches.max(axis=3).reshape(B, C * K, oh, ow)
    feat = np.concatenate([x1, x2, x3], axis=1).reshape(B, IN, oh * ow)
    y = (unpack_weight(conv_w_words, conv_w_scales, FMT).T @ mxq(feat, 1, "e4m3")).reshape(B, OUT, oh, ow)
    inv = (f64(bn_gamma) / np.sqrt(f64(bn_var) + BN_EPS))[None, :, None, None]
    y = (y - f64(bn_mean)[None, :, None, None]) * inv + f64(bn_beta)[None, :, None, None]
    y = np.maximum(y, 0.0)
    w = y.reshape(B, C, KK, NEW, NEW, oh, ow)
    px = patches.reshape(B, C, KK, 1, 1, oh, ow)
    out = np.mean(px * w, axis=2)
    out = out.transpose(0, 1, 4, 2, 5, 3)
    out = out.reshape(B, C, oh * NEW, ow * NEW)
    return out[:, :, :W, :H]

@@ -1,0 +1,310 @@
+import concourse.mybir as mybir
+from concourse.masks import make_identity
+
+F32 = mybir.dt.float32
+BF16 = mybir.dt.bfloat16
+I32 = mybir.dt.int32
+U8 = mybir.dt.uint8
+FP8X4 = mybir.dt.float8_e4m3fn_x4
+ALU = mybir.AluOpType
+ACT = mybir.ActivationFunctionType
+AX = mybir.AxisListType
+
+P = 128
+CH = 124
+LEAD = P - CH
+IMG = 32
+PAD = 3
+PIMG = IMG + 2 * PAD
+WIN = 8
+HALF_ROWS = PIMG // 2
+OHW = 16
+POS = OHW * OHW
+HALVES = POS // P
+KK = WIN * WIN
+FEATS = 2 * WIN * CH + KK
+PASSES = FEATS // (4 * P)
+OUTS = CH * KK
+TILES = OUTS // P
+ROUND = 4
+BN_EPS = 1e-5
+W_BUFS = 12
+
+FLOPS = 2 * FEATS * OUTS * POS
+
+
+def tile_revolutionnaive_w_kernel(
+    tc, x, conv_w_words, conv_w_scales, bn_gamma, bn_beta, bn_mean, bn_var, out
+):
+    nc = tc.nc
+    with tc.tile_pool(name="keep", bufs=1) as keep, tc.tile_pool(
+        name="weights", bufs=W_BUFS
+    ) as weights, tc.tile_pool(name="zpool", bufs=2 * ROUND) as zpool, tc.tile_pool(
+        name="prods", bufs=3
+    ) as prods, tc.psum_pool(name="psum", bufs=4) as psum:
+        ident_f32 = keep.tile([P, P], F32)
+        make_identity(nc, ident_f32[:])
+        ident_bf16 = keep.tile([P, P], BF16)
+        make_identity(nc, ident_bf16[:])
+
+        xs = keep.tile([P, IMG * IMG], BF16)
+        nc.vector.memset(xs[0:LEAD, :], 0.0)
+        x_rows = x.rearrange("b c r s -> (b c) (r s)")
+        first = 0
+        for size in (64, 32, 16, 8, 4):
+            nc.sync.dma_start(
+                out=xs[LEAD + first : LEAD + first + size, :], in_=x_rows[first : first + size, :]
+            )
+            first += size
+
+        rows_a = keep.tile([P, P], BF16)
+        rows_b = keep.tile([P, P], BF16)
+        nc.vector.memset(rows_a[:], 0.0)
+        nc.vector.memset(rows_b[:], 0.0)
+        nc.scalar.dma_start(out=rows_a[0:TILES, :], in_=bn_gamma.rearrange("(t p) -> t p", p=P))
+        nc.scalar.dma_start(out=rows_a[TILES : 2 * TILES, :], in_=bn_var.rearrange("(t p) -> t p", p=P))
+        nc.scalar.dma_start(out=rows_b[0:TILES, :], in_=bn_beta.rearrange("(t p) -> t p", p=P))
+        nc.scalar.dma_start(out=rows_b[TILES : 2 * TILES, :], in_=bn_mean.rearrange("(t p) -> t p", p=P))
+
+        w_planes = keep.tile([P, OUTS], U8, align_bytes=64)
+        nc.vector.memset(w_planes[:].bitcast(I32), 0)
+        for quad in range(4):
+            nc.sync.dma_start(
+                out=w_planes[32 * quad : 32 * quad + 16, :].bitcast(I32),
+                in_=conv_w_scales[:, 4 * quad : 4 * quad + 4, :].bitcast(I32),
+            )
+
+        xp = keep.tile([P, PIMG, PIMG], BF16)
+        nc.vector.memset(xp[:], 0.0)
+        out_t = keep.tile([P, HALVES, P], F32)
+        nc.vector.memset(out_t[:], 0.0)
+
+        cols_a = keep.tile([P, P], F32)
+        cols_b = keep.tile([P, P], F32)
+        for rows, cols in ((rows_a, cols_a), (rows_b, cols_b)):
+            flipped = psum.tile([P, P], BF16, tag="tp")
+            nc.tensor.transpose(flipped[:], rows[:], ident_bf16[:])
+            nc.vector.tensor_copy(out=cols[:], in_=flipped[:])
+        gamma, var = cols_a[:, 0:TILES], cols_a[:, TILES : 2 * TILES]
+        beta, mean = cols_b[:, 0:TILES], cols_b[:, TILES : 2 * TILES]
+        bn_scale = keep.tile([P, TILES], F32)
+        bn_shift = keep.tile([P, TILES], F32)
+        nc.scalar.activation(out=bn_scale[:], in_=var, func=ACT.Sqrt, bias=BN_EPS, scale=1.0)
+        nc.vector.reciprocal(out=bn_scale[:], in_=bn_scale[:])
+        nc.vector.tensor_mul(out=bn_scale[:], in0=bn_scale[:], in1=gamma)
+        nc.vector.tensor_mul(out=bn_shift[:], in0=mean, in1=bn_scale[:])
+        nc.vector.tensor_sub(out=bn_shift[:], in0=beta, in1=bn_shift[:])
+
+        xs_words = xs[:].bitcast(F32)
+        by_pixel = psum.tile([P, 4, P], F32, tag="tp")
+        for b in range(4):
+            nc.tensor.transpose(by_pixel[:, b, :], xs_words[:, P * b : P * (b + 1)], ident_f32[:])
+        pixel_max = keep.tile([P, 4, 2], BF16)
+        with nc.allow_low_precision(reason="a maximum of bfloat16 values is a bfloat16 value"):
+            nc.vector.tensor_reduce(
+                out=pixel_max[:],
+                in_=by_pixel[:].bitcast(BF16).rearrange("p b (q e) -> p b e q", e=2)[:, :, :, LEAD:P],
+                axis=AX.X,
+                op=ALU.max,
+            )
+
+        nc.vector.tensor_copy(
+            out=xp[:, PAD : PAD + IMG, PAD : PAD + IMG],
+            in_=xs[:].rearrange("q (r s) -> q r s", s=IMG),
+        )
+
+        rows2 = keep.tile([P, HALF_ROWS, PIMG], BF16)
+        rows4 = keep.tile([P, HALF_ROWS - 1, PIMG], BF16)
+        xp_row_pairs = xp[:].rearrange("q (a two) s -> q a two s", two=2)
+        nc.vector.tensor_max(out=rows2[:], in0=xp_row_pairs[:, :, 0, :], in1=xp_row_pairs[:, :, 1, :])
+        nc.vector.tensor_max(out=rows4[:], in0=rows2[:, 0 : HALF_ROWS - 1, :], in1=rows2[:, 1:HALF_ROWS, :])
+        x2_win = keep.tile([P, 4, OHW, IMG], BF16)
+        for jp in range(4):
+            nc.vector.tensor_max(
+                out=x2_win[:, jp, :, :],
+                in0=rows4[:, 0:OHW, 2 * jp : 2 * jp + IMG],
+                in1=rows4[:, 2 : OHW + 2, 2 * jp : 2 * jp + IMG],
+            )
+        cols2 = keep.tile([P, PIMG, HALF_ROWS], BF16)
+        cols4 = keep.tile([P, PIMG, HALF_ROWS - 1], BF16)
+        xp_col_pairs = xp[:].rearrange("q r (b two) -> q r b two", two=2)
+        nc.vector.tensor_max(out=cols2[:], in0=xp_col_pairs[:, :, :, 0], in1=xp_col_pairs[:, :, :, 1])
+        nc.vector.tensor_max(out=cols4[:], in0=cols2[:, :, 0 : HALF_ROWS - 1], in1=cols2[:, :, 1:HALF_ROWS])
+        x3_win = keep.tile([P, HALF_ROWS, OHW, 2], BF16)
+        cols4_pairs = cols4[:].rearrange("q (a e) b -> q a b e", e=2)
+        nc.vector.tensor_max(
+            out=x3_win[:], in0=cols4_pairs[:, :, 0:OHW, :], in1=cols4_pairs[:, :, 2 : OHW + 2, :]
+        )
+
+        for bh in range(2):
+            spread = psum.tile([P, 2, P, 2], F32, tag="tp")
+            for bl in range(2):
+                for e in range(2):
+                    nc.tensor.matmul(
+                        out=spread[:, bl, :, e],
+                        lhsT=pixel_max[:, 2 * bh + bl, e : e + 1].to_broadcast([P, P]),
+                        rhs=ident_bf16[:],
+                        start=True,
+                        stop=True,
+                    )
+            dst = xp[0:LEAD, PAD + OHW * bh : PAD + OHW * (bh + 1), PAD : PAD + IMG]
+            src = spread[0:LEAD].rearrange("q bl w e -> q (bl w e)").rearrange("q (r s) -> q r s", s=IMG)
+            if bh == 0:
+                nc.vector.tensor_copy(out=dst, in_=src)
+            else:
+                nc.scalar.copy(out=dst, in_=src)
+
+        patch_win = keep.tile([P, 2, 4, HALF_ROWS, IMG], BF16)
+        xp_by_parity = xp[:].rearrange("q (a ip) s -> q a ip s", ip=2)
+        for ip in range(2):
+            for jp in range(4):
+                dst = patch_win[:, ip, jp, :, :]
+                src = xp_by_parity[:, :, ip, 2 * jp : 2 * jp + IMG]
+                if jp % 2 == 0:
+                    nc.vector.tensor_copy(out=dst, in_=src)
+                else:
+                    nc.scalar.copy(out=dst, in_=src)
+
+        feat_t = keep.tile([P, HALVES, FEATS], BF16)
+        patches = keep.tile([P, HALVES, P, KK], BF16)
+        feat_t_words = feat_t[:].bitcast(F32)
+        patch_words = patches[:].bitcast(F32).rearrange("p h q (i jp) -> p h q i jp", jp=4)
+        x2_words = x2_win[:].rearrange("q jp u w -> q jp (u w)").bitcast(F32)
+        x3_words = x3_win[:].rearrange("q a v e -> q (a v e)").bitcast(F32)
+        win_words = patch_win[:].rearrange("q ip jp a w -> q ip jp (a w)").bitcast(F32)
+
+        def flip_four(sources, dst, first_q, h):
+            bank = psum.tile([P, 4, P], F32, tag="tp")
+            for f in range(4):
+                nc.tensor.transpose(bank[:, f, :], sources[f], ident_f32[:])
+            src = bank[:, :, first_q:P].rearrange("p f q -> p q f")
+            if h == 0:
+                nc.vector.tensor_copy(out=dst, in_=src)
+            else:
+                nc.scalar.copy(out=dst, in_=src)
+
+        x2_first = KK // 2
+        x3_first = x2_first + 4 * CH
+        for h in range(HALVES):
+            flip_four(
+                [x2_words[:, jp, P * h : P * (h + 1)] for jp in range(4)],
+                feat_t_words[:, h, x2_first:x3_first].rearrange("p (c f) -> p c f", f=4),
+                LEAD,
+                h,
+            )
+        for h in range(HALVES):
+            flip_four(
+                [x3_words[:, OHW * a + P * h : OHW * a + P * (h + 1)] for a in range(4)],
+                feat_t_words[:, h, x3_first : x3_first + 4 * CH].rearrange("p (c f) -> p c f", f=4),
+                LEAD,
+                h,
+            )
+        for i in range(WIN):
+            for h in range(HALVES):
+                start = OHW * (i // 2) + P * h
+                flip_four(
+                    [win_words[:, i % 2, jp, start : start + P] for jp in range(4)],
+                    patch_words[:, h, :, i, :],
+                    0,
+                    h,
+                )
+        nc.vector.tensor_copy(
+            out=feat_t_words[:, :, 0:x2_first],
+            in_=patches[:].bitcast(F32)[:, :, 0, :],
+        )
+
+        grouped = keep.tile([P, PASSES, 4 * POS], BF16, align_bytes=64)
+        f_codes = keep.tile([P, PASSES, POS], I32, align_bytes=64)
+        f_planes = keep.tile([P, PASSES, POS], U8, align_bytes=64)
+        grouped_words = grouped[:].bitcast(F32)
+        for g in range(PASSES):
+            bank = psum.tile([P, 2, HALVES, P], F32, tag="tp")
+            for u in range(2):
+                for h in range(HALVES):
+                    nc.tensor.transpose(
+                        bank[:, u, h, :], feat_t_words[:, h, 256 * g + u : 256 * (g + 1) : 2], ident_f32[:]
+                    )
+            dst = grouped_words[:, g, :].rearrange("p (n u) -> p n u", u=2)
+            src = bank[:].rearrange("p u h n -> p (h n) u")
+            if g % 2 == 0:
+                nc.vector.tensor_copy(out=dst, in_=src)
+            else:
+                nc.scalar.copy(out=dst, in_=src)
+        for g in range(PASSES):
+            nc.vector.quantize_mx(
+                out=f_codes[:, g, :].bitcast(FP8X4), scales=f_planes[:, g, :], in_=grouped[:, g, :]
+            )
+
+        w_words = conv_w_words.rearrange("g p n t -> p g (n t)")
+        rounds = [(t0, min(ROUND, TILES - t0)) for t0 in range(0, TILES, ROUND)]
+        z_of_round = {}
+
+        def multiply(r):
+            t0, count = rounds[r]
+            chunk = weights.tile([P, PASSES, ROUND * P], I32, align_bytes=64)
+            nc.sync.dma_start(
+                out=chunk[:, :, 0 : count * P],
+                in_=w_words[:, :, 4 * P * t0 : 4 * P * (t0 + count)].bitcast(I32),
+            )
+            z_of_round[r] = []
+            for a in range(count):
+                t = t0 + a
+                acc = psum.tile([P, POS], F32, tag="mx")
+                for g in range(PASSES):
+                    nc.tensor.matmul_mx(
+                        out=acc[:],
+                        lhsT=chunk[:, g, P * a : P * (a + 1)].bitcast(FP8X4),
+                        lhsT_scale=w_planes[4 * g : P, P * t : P * (t + 1)],
+                        rhs=f_codes[:, g, :].bitcast(FP8X4),
+                        rhs_scale=f_planes[:, g, :],
+                        start=(g == 0),
+                        stop=(g == PASSES - 1),
+                    )
+                z = zpool.tile([P, POS], F32, tag="z")
+                nc.scalar.activation(
+                    out=z[:], in_=acc[:], func=ACT.Relu, bias=bn_shift[:, t : t + 1], scale=bn_scale[:, t : t + 1]
+                )
+                z_of_round[r].append(z)
+
+        def apply_to_patches(r):
+            t0, count = rounds[r]
+            q0 = LEAD + 2 * t0
+            for h in range(HALVES):
+                z_t = psum.tile([P, ROUND * P], F32, tag="tp")
+                for a in range(count):
+                    nc.tensor.transpose(
+                        z_t[:, P * a : P * (a + 1)], z_of_round[r][a][:, P * h : P * (h + 1)], ident_f32[:]
+                    )
+                prod = prods.tile([P, ROUND * P], F32, tag="prod")
+                nc.vector.tensor_mul(
+                    out=prod[:, 0 : count * P],
+                    in0=z_t[:, 0 : count * P],
+                    in1=patches[:, h, q0 : q0 + 2 * count, :].rearrange("p q k -> p (q k)"),
+                )
+                nc.vector.tensor_reduce(
+                    out=out_t[:, h, q0 : q0 + 2 * count],
+                    in_=prod[:, 0 : count * P].rearrange("p (q k) -> p q k", k=KK),
+                    axis=AX.X,
+                    op=ALU.add,
+                )
+
+        for r in range(len(rounds) + 1):
+            if r < len(rounds):
+                multiply(r)
+            if r > 0:
+                apply_to_patches(r - 1)
+
+        by_channel = psum.tile([P, HALVES, P], F32, tag="tp")
+        for h in range(HALVES):
+            nc.tensor.transpose(by_channel[:, h, :], out_t[:, h, :], ident_f32[:])
+        result = keep.tile([P, POS], F32)
+        nc.vector.tensor_scalar_mul(
+            out=result[:], in0=by_channel[:].rearrange("q h n -> q (h n)"), scalar1=1.0 / KK
+        )
+        out_rows = out.rearrange("b c u v -> (b c) (u v)")
+        first = 0
+        for size in (64, 32, 16, 8, 4):
+            nc.sync.dma_start(
+                out=out_rows[first : first + size, :], in_=result[LEAD + first : LEAD + first + size, :]
+            )
+            first += size

@@ -15,12 +15,15 @@ CH = 124
 LEAD = P - CH
 IMG = 32
 PAD = 3
-PIMG = IMG + 2 * PAD
+PCOLS = IMG + 2 * PAD
+PROWS = 40
 WIN = 8
-HALF_ROWS = PIMG // 2
+HALF_ROWS = 19
 OHW = 16
 POS = OHW * OHW
-HALVES = POS // P
+HALVES = 2
+U2 = OHW // 2
+WROWS = WIN + 2
 KK = WIN * WIN
 FEATS = 2 * WIN * CH + KK
 PASSES = FEATS // (4 * P)
@@ -29,6 +32,7 @@ TILES = OUTS // P
 ROUND = 4
 BN_EPS = 1e-5
 W_BUFS = 12
+FLIP_AFTER = 1
 
 FLOPS = 2 * FEATS * OUTS * POS
 
@@ -39,13 +43,19 @@ def tile_revolutionnaive_w_kernel(
     nc = tc.nc
     with tc.tile_pool(name="keep", bufs=1) as keep, tc.tile_pool(
         name="weights", bufs=W_BUFS
-    ) as weights, tc.tile_pool(name="zpool", bufs=2 * ROUND) as zpool, tc.tile_pool(
+    ) as weights, tc.tile_pool(name="zpool", bufs=4 * ROUND) as zpool, tc.tile_pool(
         name="prods", bufs=3
-    ) as prods, tc.psum_pool(name="psum", bufs=4) as psum:
-        ident_f32 = keep.tile([P, P], F32)
-        make_identity(nc, ident_f32[:])
-        ident_bf16 = keep.tile([P, P], BF16)
-        make_identity(nc, ident_bf16[:])
+    ) as prods, tc.psum_pool(name="psum", bufs=4) as psum, tc.manual_schedule(
+        engines={mybir.EngineType.SP}
+    ):
+        rows_a = keep.tile([P, P], BF16)
+        rows_b = keep.tile([P, P], BF16)
+        nc.vector.memset(rows_a[:], 0.0)
+        nc.vector.memset(rows_b[:], 0.0)
+        nc.scalar.dma_start(out=rows_a[0:TILES, :], in_=bn_gamma.rearrange("(t p) -> t p", p=P))
+        nc.scalar.dma_start(out=rows_a[TILES : 2 * TILES, :], in_=bn_var.rearrange("(t p) -> t p", p=P))
+        nc.scalar.dma_start(out=rows_b[0:TILES, :], in_=bn_beta.rearrange("(t p) -> t p", p=P))
+        nc.scalar.dma_start(out=rows_b[TILES : 2 * TILES, :], in_=bn_mean.rearrange("(t p) -> t p", p=P))
 
         xs = keep.tile([P, IMG * IMG], BF16)
         nc.vector.memset(xs[0:LEAD, :], 0.0)
@@ -56,28 +66,165 @@ def tile_revolutionnaive_w_kernel(
                 out=xs[LEAD + first : LEAD + first + size, :], in_=x_rows[first : first + size, :]
             )
             first += size
-
-        rows_a = keep.tile([P, P], BF16)
-        rows_b = keep.tile([P, P], BF16)
-        nc.vector.memset(rows_a[:], 0.0)
-        nc.vector.memset(rows_b[:], 0.0)
-        nc.scalar.dma_start(out=rows_a[0:TILES, :], in_=bn_gamma.rearrange("(t p) -> t p", p=P))
-        nc.scalar.dma_start(out=rows_a[TILES : 2 * TILES, :], in_=bn_var.rearrange("(t p) -> t p", p=P))
-        nc.scalar.dma_start(out=rows_b[0:TILES, :], in_=bn_beta.rearrange("(t p) -> t p", p=P))
-        nc.scalar.dma_start(out=rows_b[TILES : 2 * TILES, :], in_=bn_mean.rearrange("(t p) -> t p", p=P))
-
+        xp = keep.tile([P, PROWS, PCOLS], BF16)
+        nc.vector.memset(xp[:], 0.0)
+        feat_t = keep.tile([P, HALVES, 2, FEATS // 2], BF16)
+        feat_words = feat_t[:].bitcast(F32)
+        x2_first = KK // 4
+        x3_first = x2_first + 2 * CH
+        nc.vector.memset(feat_t[:, :, :, 0 : 2 * x2_first], 0.0)
+        cm_rows = keep.tile([P, PCOLS], BF16)
+        nc.vector.memset(cm_rows[:], 0.0)
         w_planes = keep.tile([P, OUTS], U8, align_bytes=64)
         nc.vector.memset(w_planes[:].bitcast(I32), 0)
+
+        warm = keep.tile([P, 1], F32)
+        nc.gpsimd.memset(warm[:], 1.0)
+        nc.scalar.activation(out=warm[:], in_=warm[:], func=ACT.Sqrt)
+
+        ident_f32 = keep.tile([P, P], F32)
+        make_identity(nc, ident_f32[:])
+        ident_bf16 = keep.tile([P, P], BF16)
+        make_identity(nc, ident_bf16[:])
+        every_fourth = keep.tile([P, 768], BF16)
+        nc.gpsimd.memset(every_fourth[:], 0.0)
+        nc.gpsimd.tensor_copy(out=every_fourth[:, 268 : 268 + P], in_=ident_bf16[:])
+        two_blocks = keep.tile([P, 94, 2], BF16)
+        nc.gpsimd.memset(two_blocks[:], 0.0)
+        nc.gpsimd.tensor_copy(out=two_blocks[:, :, 0], in_=ident_bf16[:, 0:94])
+        nc.gpsimd.tensor_copy(out=two_blocks[:, 0:64, 1], in_=ident_bf16[:, 64:P])
+        two_blocks_flat = two_blocks[:].rearrange("k c two -> k (c two)")
+
         for quad in range(4):
             nc.sync.dma_start(
                 out=w_planes[32 * quad : 32 * quad + 16, :].bitcast(I32),
                 in_=conv_w_scales[:, 4 * quad : 4 * quad + 4, :].bitcast(I32),
             )
 
-        xp = keep.tile([P, PIMG, PIMG], BF16)
-        nc.vector.memset(xp[:], 0.0)
         out_t = keep.tile([P, HALVES, P], F32)
-        nc.vector.memset(out_t[:], 0.0)
+        nc.gpsimd.memset(out_t[:], 0.0)
+
+        banks_made = []
+
+        def early_bank(shape):
+            banks_made.append(1)
+            if len(banks_made) % 2 == 0:
+                bank = psum.tile(shape, F32, tag="mx")
+            else:
+                bank = psum.tile(shape, F32, tag="tp")
+            return bank
+
+        def copy_on(engine, dst, src):
+            if engine == "v":
+                nc.vector.tensor_copy(out=dst, in_=src)
+            else:
+                nc.scalar.copy(out=dst, in_=src)
+
+        grouped = keep.tile([P, PASSES, 4 * POS], BF16, align_bytes=64)
+        f_codes = keep.tile([P, PASSES, POS], I32, align_bytes=64)
+        f_planes = keep.tile([P, PASSES, POS], U8, align_bytes=64)
+        grouped_words = grouped[:].bitcast(F32)
+
+        xs_words = xs[:].bitcast(F32)
+        by_pixel = early_bank([P, 4, P])
+        for b in range(4):
+            nc.tensor.transpose(by_pixel[:, b, :], xs_words[:, b : 4 * P : 4], ident_f32[:])
+        nc.scalar.copy(
+            out=xp[:, PAD : PAD + IMG, PAD : PAD + IMG],
+            in_=xs[:].rearrange("q (r s) -> q r s", s=IMG),
+        )
+        pixel_max = keep.tile([P, 4, 2], BF16)
+        with nc.allow_low_precision(reason="a maximum of bfloat16 values is a bfloat16 value"):
+            nc.vector.tensor_reduce(
+                out=pixel_max[:],
+                in_=by_pixel[:].bitcast(BF16).rearrange("p b (q e) -> p b e q", e=2)[:, :, :, LEAD:P],
+                axis=AX.X,
+                op=ALU.max,
+            )
+        row_image = early_bank([P, IMG])
+        for a in range(4):
+            for fh in range(2):
+                nc.tensor.matmul(
+                    out=row_image[:, 8 * a : 8 * (a + 1)],
+                    lhsT=every_fourth[:, a + 256 * (1 - fh) : a + 256 * (1 - fh) + 4 * (P - 1) + 1 : 4],
+                    rhs=pixel_max[:].rearrange("p b e -> p (b e)"),
+                    start=(fh == 0),
+                    stop=(fh == 1),
+                )
+        nc.scalar.copy(out=cm_rows[0:64, PAD : PAD + IMG], in_=row_image[0:64, :])
+        nc.scalar.copy(out=cm_rows[64:P, 0 : IMG - 1], in_=row_image[64:P, 1:IMG])
+        x1_rows = keep.tile([P, 4 * POS], BF16)
+        for h in range(HALVES):
+            x1_bank = early_bank([P, U2, OHW, 4])
+            for u2 in range(U2):
+                shift = 2 * (4 * u2 + 2 * h)
+                for th in range(2):
+                    nc.tensor.matmul(
+                        out=x1_bank[:, u2, :, 2 * th : 2 * th + 2],
+                        lhsT=two_blocks_flat[:, shift : shift + P],
+                        rhs=cm_rows[:, 2 * th : 2 * th + 2 * OHW].rearrange("k (v two) -> k v two", two=2),
+                        start=True,
+                        stop=True,
+                    )
+            nc.scalar.copy(
+                out=x1_rows[0:x2_first, 4 * P * h : 4 * P * (h + 1)],
+                in_=x1_bank[0:x2_first].rearrange("k u2 v t -> k (u2 v t)"),
+            )
+
+        def flip_four(sources, bank):
+            for f in range(4):
+                nc.tensor.transpose(bank[:, f, :], sources[f], ident_f32[:])
+
+        def flip_features(sources, h, first_n, engine):
+            bank = early_bank([P, 4, P])
+            flip_four(sources, bank)
+            copy_on(
+                engine,
+                feat_words[:, h, :, first_n : first_n + 2 * CH].rearrange("p e (c fh) -> p e c fh", fh=2),
+                bank[:, :, LEAD:P].rearrange("p (fh e) c -> p e c fh", e=2),
+            )
+
+        rows2 = keep.tile([P, HALF_ROWS, PCOLS], BF16)
+        rows4 = keep.tile([P, HALF_ROWS - 1, PCOLS], BF16)
+        rows8 = keep.tile([P, OHW, PCOLS], BF16)
+        xp_row_pairs = xp[:, 0 : 2 * HALF_ROWS, :].rearrange("q (a two) s -> q a two s", two=2)
+        nc.vector.tensor_max(out=rows2[:], in0=xp_row_pairs[:, :, 0, :], in1=xp_row_pairs[:, :, 1, :])
+        nc.vector.tensor_max(out=rows4[:], in0=rows2[:, 0 : HALF_ROWS - 1, :], in1=rows2[:, 1:HALF_ROWS, :])
+        nc.vector.tensor_max(out=rows8[:], in0=rows4[:, 0:OHW, :], in1=rows4[:, 2 : OHW + 2, :])
+        x2_win = keep.tile([P, 4, HALVES, U2, IMG], BF16)
+        for jp in range(4):
+            nc.scalar.copy(
+                out=x2_win[:, jp, :, :, :].rearrange("q h u2 w -> q u2 h w"),
+                in_=rows8[:, :, 2 * jp : 2 * jp + IMG].rearrange("q (u2 h) w -> q u2 h w", h=HALVES),
+            )
+        x2_words = x2_win[:].rearrange("q jp h u2 w -> q jp h (u2 w)").bitcast(F32)
+        for h in range(HALVES):
+            flip_features([x2_words[:, jp, h, :] for jp in range(4)], h, x2_first, "s")
+
+        cols2 = keep.tile([P, PROWS, HALF_ROWS], BF16)
+        cols4 = keep.tile([P, PROWS, HALF_ROWS - 1], BF16)
+        xp_col_pairs = xp[:].rearrange("q r (b two) -> q r b two", two=2)
+        nc.vector.tensor_max(out=cols2[:], in0=xp_col_pairs[:, :, :, 0], in1=xp_col_pairs[:, :, :, 1])
+        nc.vector.tensor_max(out=cols4[:], in0=cols2[:, :, 0 : HALF_ROWS - 1], in1=cols2[:, :, 1:HALF_ROWS])
+        x3_win = keep.tile([P, 2, PROWS // 4, OHW, 2], BF16)
+        cols4_by_four = cols4[:].rearrange("q (a par e) b -> q par a b e", par=2, e=2)
+        for par in range(2):
+            nc.vector.tensor_max(
+                out=x3_win[:, par, :, :, :],
+                in0=cols4_by_four[:, par, :, 0:OHW, :],
+                in1=cols4_by_four[:, par, :, 2 : OHW + 2, :],
+            )
+        x3_words = x3_win[:].rearrange("q par a v e -> q par (a v e)").bitcast(F32)
+        for h in range(HALVES):
+            flip_features(
+                [
+                    x3_words[:, (h + ip) % 2, OHW * ((h + ip) // 2) : OHW * ((h + ip) // 2) + P]
+                    for ip in range(4)
+                ],
+                h,
+                x3_first,
+                "v",
+            )
 
         cols_a = keep.tile([P, P], F32)
         cols_b = keep.tile([P, P], F32)
@@ -95,145 +242,37 @@ def tile_revolutionnaive_w_kernel(
         nc.vector.tensor_mul(out=bn_shift[:], in0=mean, in1=bn_scale[:])
         nc.vector.tensor_sub(out=bn_shift[:], in0=beta, in1=bn_shift[:])
 
-        xs_words = xs[:].bitcast(F32)
-        by_pixel = psum.tile([P, 4, P], F32, tag="tp")
-        for b in range(4):
-            nc.tensor.transpose(by_pixel[:, b, :], xs_words[:, P * b : P * (b + 1)], ident_f32[:])
-        pixel_max = keep.tile([P, 4, 2], BF16)
-        with nc.allow_low_precision(reason="a maximum of bfloat16 values is a bfloat16 value"):
-            nc.vector.tensor_reduce(
-                out=pixel_max[:],
-                in_=by_pixel[:].bitcast(BF16).rearrange("p b (q e) -> p b e q", e=2)[:, :, :, LEAD:P],
-                axis=AX.X,
-                op=ALU.max,
-            )
-
-        nc.vector.tensor_copy(
-            out=xp[:, PAD : PAD + IMG, PAD : PAD + IMG],
-            in_=xs[:].rearrange("q (r s) -> q r s", s=IMG),
-        )
-
-        rows2 = keep.tile([P, HALF_ROWS, PIMG], BF16)
-        rows4 = keep.tile([P, HALF_ROWS - 1, PIMG], BF16)
-        xp_row_pairs = xp[:].rearrange("q (a two) s -> q a two s", two=2)
-        nc.vector.tensor_max(out=rows2[:], in0=xp_row_pairs[:, :, 0, :], in1=xp_row_pairs[:, :, 1, :])
-        nc.vector.tensor_max(out=rows4[:], in0=rows2[:, 0 : HALF_ROWS - 1, :], in1=rows2[:, 1:HALF_ROWS, :])
-        x2_win = keep.tile([P, 4, OHW, IMG], BF16)
-        for jp in range(4):
-            nc.vector.tensor_max(
-                out=x2_win[:, jp, :, :],
-                in0=rows4[:, 0:OHW, 2 * jp : 2 * jp + IMG],
-                in1=rows4[:, 2 : OHW + 2, 2 * jp : 2 * jp + IMG],
-            )
-        cols2 = keep.tile([P, PIMG, HALF_ROWS], BF16)
-        cols4 = keep.tile([P, PIMG, HALF_ROWS - 1], BF16)
-        xp_col_pairs = xp[:].rearrange("q r (b two) -> q r b two", two=2)
-        nc.vector.tensor_max(out=cols2[:], in0=xp_col_pairs[:, :, :, 0], in1=xp_col_pairs[:, :, :, 1])
-        nc.vector.tensor_max(out=cols4[:], in0=cols2[:, :, 0 : HALF_ROWS - 1], in1=cols2[:, :, 1:HALF_ROWS])
-        x3_win = keep.tile([P, HALF_ROWS, OHW, 2], BF16)
-        cols4_pairs = cols4[:].rearrange("q (a e) b -> q a b e", e=2)
-        nc.vector.tensor_max(
-            out=x3_win[:], in0=cols4_pairs[:, :, 0:OHW, :], in1=cols4_pairs[:, :, 2 : OHW + 2, :]
-        )
-
-        for bh in range(2):
-            spread = psum.tile([P, 2, P, 2], F32, tag="tp")
-            for bl in range(2):
-                for e in range(2):
-                    nc.tensor.matmul(
-                        out=spread[:, bl, :, e],
-                        lhsT=pixel_max[:, 2 * bh + bl, e : e + 1].to_broadcast([P, P]),
-                        rhs=ident_bf16[:],
-                        start=True,
-                        stop=True,
-                    )
-            dst = xp[0:LEAD, PAD + OHW * bh : PAD + OHW * (bh + 1), PAD : PAD + IMG]
-            src = spread[0:LEAD].rearrange("q bl w e -> q (bl w e)").rearrange("q (r s) -> q r s", s=IMG)
-            if bh == 0:
-                nc.vector.tensor_copy(out=dst, in_=src)
-            else:
-                nc.scalar.copy(out=dst, in_=src)
-
-        patch_win = keep.tile([P, 2, 4, HALF_ROWS, IMG], BF16)
-        xp_by_parity = xp[:].rearrange("q (a ip) s -> q a ip s", ip=2)
-        for ip in range(2):
-            for jp in range(4):
-                dst = patch_win[:, ip, jp, :, :]
-                src = xp_by_parity[:, :, ip, 2 * jp : 2 * jp + IMG]
-                if jp % 2 == 0:
-                    nc.vector.tensor_copy(out=dst, in_=src)
-                else:
-                    nc.scalar.copy(out=dst, in_=src)
-
-        feat_t = keep.tile([P, HALVES, FEATS], BF16)
-        patches = keep.tile([P, HALVES, P, KK], BF16)
-        feat_t_words = feat_t[:].bitcast(F32)
-        patch_words = patches[:].bitcast(F32).rearrange("p h q (i jp) -> p h q i jp", jp=4)
-        x2_words = x2_win[:].rearrange("q jp u w -> q jp (u w)").bitcast(F32)
-        x3_words = x3_win[:].rearrange("q a v e -> q (a v e)").bitcast(F32)
-        win_words = patch_win[:].rearrange("q ip jp a w -> q ip jp (a w)").bitcast(F32)
-
-        def flip_four(sources, dst, first_q, h):
-            bank = psum.tile([P, 4, P], F32, tag="tp")
-            for f in range(4):
-                nc.tensor.transpose(bank[:, f, :], sources[f], ident_f32[:])
-            src = bank[:, :, first_q:P].rearrange("p f q -> p q f")
-            if h == 0:
-                nc.vector.tensor_copy(out=dst, in_=src)
-            else:
-                nc.scalar.copy(out=dst, in_=src)
-
-        x2_first = KK // 2
-        x3_first = x2_first + 4 * CH
-        for h in range(HALVES):
-            flip_four(
-                [x2_words[:, jp, P * h : P * (h + 1)] for jp in range(4)],
-                feat_t_words[:, h, x2_first:x3_first].rearrange("p (c f) -> p c f", f=4),
-                LEAD,
-                h,
-            )
-        for h in range(HALVES):
-            flip_four(
-                [x3_words[:, OHW * a + P * h : OHW * a + P * (h + 1)] for a in range(4)],
-                feat_t_words[:, h, x3_first : x3_first + 4 * CH].rearrange("p (c f) -> p c f", f=4),
-                LEAD,
-                h,
-            )
-        for i in range(WIN):
-            for h in range(HALVES):
-                start = OHW * (i // 2) + P * h
-                flip_four(
-                    [win_words[:, i % 2, jp, start : start + P] for jp in range(4)],
-                    patch_words[:, h, :, i, :],
-                    0,
-                    h,
-                )
-        nc.vector.tensor_copy(
-            out=feat_t_words[:, :, 0:x2_first],
-            in_=patches[:].bitcast(F32)[:, :, 0, :],
-        )
-
-        grouped = keep.tile([P, PASSES, 4 * POS], BF16, align_bytes=64)
-        f_codes = keep.tile([P, PASSES, POS], I32, align_bytes=64)
-        f_planes = keep.tile([P, PASSES, POS], U8, align_bytes=64)
-        grouped_words = grouped[:].bitcast(F32)
-        for g in range(PASSES):
-            bank = psum.tile([P, 2, HALVES, P], F32, tag="tp")
-            for u in range(2):
+        for g in (1, 0, 3, 2):
+            bank = early_bank([P, 2, HALVES, P])
+            for e in range(2):
                 for h in range(HALVES):
-                    nc.tensor.transpose(
-                        bank[:, u, h, :], feat_t_words[:, h, 256 * g + u : 256 * (g + 1) : 2], ident_f32[:]
-                    )
-            dst = grouped_words[:, g, :].rearrange("p (n u) -> p n u", u=2)
-            src = bank[:].rearrange("p u h n -> p (h n) u")
-            if g % 2 == 0:
-                nc.vector.tensor_copy(out=dst, in_=src)
-            else:
-                nc.scalar.copy(out=dst, in_=src)
-        for g in range(PASSES):
+                    nc.tensor.transpose(bank[:, e, h, :], feat_words[:, h, e, P * g : P * (g + 1)], ident_f32[:])
+            copy_on(
+                "ssvv"[g],
+                grouped_words[:, g, :].rearrange("p (n e) -> p n e", e=2),
+                bank[:].rearrange("p e h n -> p (h n) e"),
+            )
+            if g == 0:
+                nc.vector.tensor_copy(out=grouped[0:x2_first, 0, :], in_=x1_rows[0:x2_first, :])
+        for g in (1, 0, 3, 2):
             nc.vector.quantize_mx(
                 out=f_codes[:, g, :].bitcast(FP8X4), scales=f_planes[:, g, :], in_=grouped[:, g, :]
             )
+
+        patch_win = keep.tile([P, 4, 4, PROWS // 4, IMG], BF16)
+        xp_by_four = xp[:].rearrange("q (a rho) s -> q rho a s", rho=4)
+        for jp in range(4):
+            nc.vector.tensor_copy(out=patch_win[:, jp, :, :, :], in_=xp_by_four[:, :, :, 2 * jp : 2 * jp + IMG])
+        patches = keep.tile([P, P, WROWS, WIN], BF16)
+        patch_words = patches[:].bitcast(F32)
+        win_words = patch_win[:].rearrange("q jp rho a w -> q jp rho (a w)").bitcast(F32)
+
+        def flip_patches():
+            for r in range(WROWS):
+                start = OHW * (r // 4)
+                bank = psum.tile([P, 4, P], F32, tag="tp")
+                flip_four([win_words[:, jp, r % 4, start : start + P] for jp in range(4)], bank)
+                copy_on("vs"[r % 2], patch_words[:, :, r, :], bank[:].rearrange("p f q -> p q f"))
 
         w_words = conv_w_words.rearrange("g p n t -> p g (n t)")
         rounds = [(t0, min(ROUND, TILES - t0)) for t0 in range(0, TILES, ROUND)]
@@ -277,9 +316,9 @@ def tile_revolutionnaive_w_kernel(
                     )
                 prod = prods.tile([P, ROUND * P], F32, tag="prod")
                 nc.vector.tensor_mul(
-                    out=prod[:, 0 : count * P],
-                    in0=z_t[:, 0 : count * P],
-                    in1=patches[:, h, q0 : q0 + 2 * count, :].rearrange("p q k -> p (q k)"),
+                    out=prod[:, 0 : count * P].rearrange("p (q k) -> p q k", k=KK),
+                    in0=z_t[:, 0 : count * P].rearrange("p (q k) -> p q k", k=KK),
+                    in1=patches[:, q0 : q0 + 2 * count, 2 * h : 2 * h + WIN, :].rearrange("p q i j -> p q (i j)"),
                 )
                 nc.vector.tensor_reduce(
                     out=out_t[:, h, q0 : q0 + 2 * count],
@@ -288,18 +327,25 @@ def tile_revolutionnaive_w_kernel(
                     op=ALU.add,
                 )
 
+        applied = 0
         for r in range(len(rounds) + 1):
             if r < len(rounds):
                 multiply(r)
-            if r > 0:
-                apply_to_patches(r - 1)
+            if r == FLIP_AFTER:
+                flip_patches()
+            if r > FLIP_AFTER:
+                for late in range(applied, r):
+                    apply_to_patches(late)
+                applied = r
 
         by_channel = psum.tile([P, HALVES, P], F32, tag="tp")
         for h in range(HALVES):
             nc.tensor.transpose(by_channel[:, h, :], out_t[:, h, :], ident_f32[:])
         result = keep.tile([P, POS], F32)
         nc.vector.tensor_scalar_mul(
-            out=result[:], in0=by_channel[:].rearrange("q h n -> q (h n)"), scalar1=1.0 / KK
+            out=result[:].rearrange("q (u2 h v) -> q h u2 v", h=HALVES, v=OHW),
+            in0=by_channel[:].rearrange("q h (u2 v) -> q h u2 v", v=OHW),
+            scalar1=1.0 / KK,
         )
         out_rows = out.rearrange("b c u v -> (b c) (u v)")
         first = 0

@@ -32,7 +32,6 @@ TILES = OUTS // P
 ROUND = 4
 BN_EPS = 1e-5
 W_BUFS = 12
-FLIP_AFTER = 1
 
 FLOPS = 2 * FEATS * OUTS * POS
 
@@ -43,7 +42,7 @@ def tile_revolutionnaive_w_kernel(
     nc = tc.nc
     with tc.tile_pool(name="keep", bufs=1) as keep, tc.tile_pool(
         name="weights", bufs=W_BUFS
-    ) as weights, tc.tile_pool(name="zpool", bufs=4 * ROUND) as zpool, tc.tile_pool(
+    ) as weights, tc.tile_pool(name="zpool", bufs=3 * ROUND) as zpool, tc.tile_pool(
         name="prods", bufs=3
     ) as prods, tc.psum_pool(name="psum", bufs=4) as psum, tc.manual_schedule(
         engines={mybir.EngineType.SP}
@@ -104,14 +103,8 @@ def tile_revolutionnaive_w_kernel(
         out_t = keep.tile([P, HALVES, P], F32)
         nc.gpsimd.memset(out_t[:], 0.0)
 
-        banks_made = []
-
         def early_bank(shape):
-            banks_made.append(1)
-            if len(banks_made) % 2 == 0:
-                bank = psum.tile(shape, F32, tag="mx")
-            else:
-                bank = psum.tile(shape, F32, tag="tp")
+            bank = psum.tile(shape, F32, tag="mx")
             return bank
 
         def copy_on(engine, dst, src):
@@ -223,13 +216,18 @@ def tile_revolutionnaive_w_kernel(
                 ],
                 h,
                 x3_first,
-                "v",
+                "sv"[h],
             )
+
+        patch_win = keep.tile([P, 4, 4, PROWS // 4, IMG], BF16)
+        xp_by_four = xp[:].rearrange("q (a rho) s -> q rho a s", rho=4)
+        for jp in range(4):
+            nc.vector.tensor_copy(out=patch_win[:, jp, :, :, :], in_=xp_by_four[:, :, :, 2 * jp : 2 * jp + IMG])
 
         cols_a = keep.tile([P, P], F32)
         cols_b = keep.tile([P, P], F32)
         for rows, cols in ((rows_a, cols_a), (rows_b, cols_b)):
-            flipped = psum.tile([P, P], BF16, tag="tp")
+            flipped = psum.tile([P, P], BF16, tag="mx")
             nc.tensor.transpose(flipped[:], rows[:], ident_bf16[:])
             nc.vector.tensor_copy(out=cols[:], in_=flipped[:])
         gamma, var = cols_a[:, 0:TILES], cols_a[:, TILES : 2 * TILES]
@@ -259,20 +257,15 @@ def tile_revolutionnaive_w_kernel(
                 out=f_codes[:, g, :].bitcast(FP8X4), scales=f_planes[:, g, :], in_=grouped[:, g, :]
             )
 
-        patch_win = keep.tile([P, 4, 4, PROWS // 4, IMG], BF16)
-        xp_by_four = xp[:].rearrange("q (a rho) s -> q rho a s", rho=4)
-        for jp in range(4):
-            nc.vector.tensor_copy(out=patch_win[:, jp, :, :, :], in_=xp_by_four[:, :, :, 2 * jp : 2 * jp + IMG])
         patches = keep.tile([P, P, WROWS, WIN], BF16)
         patch_words = patches[:].bitcast(F32)
         win_words = patch_win[:].rearrange("q jp rho a w -> q jp rho (a w)").bitcast(F32)
 
-        def flip_patches():
-            for r in range(WROWS):
-                start = OHW * (r // 4)
-                bank = psum.tile([P, 4, P], F32, tag="tp")
-                flip_four([win_words[:, jp, r % 4, start : start + P] for jp in range(4)], bank)
-                copy_on("vs"[r % 2], patch_words[:, :, r, :], bank[:].rearrange("p f q -> p q f"))
+        for r in range(WROWS):
+            start = OHW * (r // 4)
+            bank = psum.tile([P, 4, P], F32, tag="tp")
+            flip_four([win_words[:, jp, r % 4, start : start + P] for jp in range(4)], bank)
+            copy_on("ssssssvvvv"[r], patch_words[:, :, r, :], bank[:].rearrange("p f q -> p q f"))
 
         w_words = conv_w_words.rearrange("g p n t -> p g (n t)")
         rounds = [(t0, min(ROUND, TILES - t0)) for t0 in range(0, TILES, ROUND)]
@@ -327,16 +320,11 @@ def tile_revolutionnaive_w_kernel(
                     op=ALU.add,
                 )
 
-        applied = 0
         for r in range(len(rounds) + 1):
             if r < len(rounds):
                 multiply(r)
-            if r == FLIP_AFTER:
-                flip_patches()
-            if r > FLIP_AFTER:
-                for late in range(applied, r):
-                    apply_to_patches(late)
-                applied = r
+            if r > 0:
+                apply_to_patches(r - 1)
 
         by_channel = psum.tile([P, HALVES, P], F32, tag="tp")
         for h in range(HALVES):

@@ -313,12 +313,22 @@ def tile_revolutionnaive_w_kernel(
                     in0=z_t[:, 0 : count * P].rearrange("p (q k) -> p q k", k=KK),
                     in1=patches[:, q0 : q0 + 2 * count, 2 * h : 2 * h + WIN, :].rearrange("p q i j -> p q (i j)"),
                 )
-                nc.vector.tensor_reduce(
-                    out=out_t[:, h, q0 : q0 + 2 * count],
-                    in_=prod[:, 0 : count * P].rearrange("p (q k) -> p q k", k=KK),
-                    axis=AX.X,
-                    op=ALU.add,
-                )
+                if h == 0:
+                    nc.vector.tensor_reduce(
+                        out=out_t[:, h, q0 : q0 + 2 * count],
+                        in_=prod[:, 0 : count * P].rearrange("p (q k) -> p q k", k=KK),
+                        axis=AX.X,
+                        op=ALU.add,
+                    )
+                else:
+                    for c in range(2 * count):
+                        unused = prods.tile([P, KK], F32, tag="unused")
+                        nc.scalar.activation(
+                            out=unused[:],
+                            in_=prod[:, KK * c : KK * (c + 1)],
+                            func=ACT.Copy,
+                            accum_out=out_t[:, h, q0 + c : q0 + c + 1],
+                        )
 
         for r in range(len(rounds) + 1):
             if r < len(rounds):

@@ -49,15 +49,15 @@ def tile_revolutionnaive_w_kernel(
     ):
         rows_a = keep.tile([P, P], BF16)
         rows_b = keep.tile([P, P], BF16)
-        nc.vector.memset(rows_a[:], 0.0)
-        nc.vector.memset(rows_b[:], 0.0)
+        nc.vector.memset(rows_a[:].bitcast(F32), 0.0)
+        nc.vector.memset(rows_b[:].bitcast(F32), 0.0)
         nc.scalar.dma_start(out=rows_a[0:TILES, :], in_=bn_gamma.rearrange("(t p) -> t p", p=P))
         nc.scalar.dma_start(out=rows_a[TILES : 2 * TILES, :], in_=bn_var.rearrange("(t p) -> t p", p=P))
         nc.scalar.dma_start(out=rows_b[0:TILES, :], in_=bn_beta.rearrange("(t p) -> t p", p=P))
         nc.scalar.dma_start(out=rows_b[TILES : 2 * TILES, :], in_=bn_mean.rearrange("(t p) -> t p", p=P))
 
         xs = keep.tile([P, IMG * IMG], BF16)
-        nc.vector.memset(xs[0:LEAD, :], 0.0)
+        nc.vector.memset(xs[0:LEAD, :].bitcast(F32), 0.0)
         x_rows = x.rearrange("b c r s -> (b c) (r s)")
         first = 0
         for size in (64, 32, 16, 8, 4):
@@ -66,14 +66,14 @@ def tile_revolutionnaive_w_kernel(
             )
             first += size
         xp = keep.tile([P, PROWS, PCOLS], BF16)
-        nc.vector.memset(xp[:], 0.0)
+        nc.vector.memset(xp[:].rearrange("q r s -> q (r s)").bitcast(F32), 0.0)
         feat_t = keep.tile([P, HALVES, 2, FEATS // 2], BF16)
         feat_words = feat_t[:].bitcast(F32)
         x2_first = KK // 4
         x3_first = x2_first + 2 * CH
-        nc.vector.memset(feat_t[:, :, :, 0 : 2 * x2_first], 0.0)
+        nc.vector.memset(feat_words[:, :, :, 0:x2_first], 0.0)
         cm_rows = keep.tile([P, PCOLS], BF16)
-        nc.vector.memset(cm_rows[:], 0.0)
+        nc.vector.memset(cm_rows[:].bitcast(F32), 0.0)
         w_planes = keep.tile([P, OUTS], U8, align_bytes=64)
         nc.vector.memset(w_planes[:].bitcast(I32), 0)
 
@@ -177,6 +177,11 @@ def tile_revolutionnaive_w_kernel(
                 bank[:, :, LEAD:P].rearrange("p (fh e) c -> p e c fh", e=2),
             )
 
+        patch_win = keep.tile([P, 4, 4, PROWS // 4, IMG], BF16)
+        xp_by_four = xp[:].rearrange("q (a rho) s -> q rho a s", rho=4)
+        for jp in range(4):
+            nc.vector.tensor_copy(out=patch_win[:, jp, :, :, :], in_=xp_by_four[:, :, :, 2 * jp : 2 * jp + IMG])
+
         rows2 = keep.tile([P, HALF_ROWS, PCOLS], BF16)
         rows4 = keep.tile([P, HALF_ROWS - 1, PCOLS], BF16)
         rows8 = keep.tile([P, OHW, PCOLS], BF16)
@@ -218,11 +223,6 @@ def tile_revolutionnaive_w_kernel(
                 x3_first,
                 "sv"[h],
             )
-
-        patch_win = keep.tile([P, 4, 4, PROWS // 4, IMG], BF16)
-        xp_by_four = xp[:].rearrange("q (a rho) s -> q rho a s", rho=4)
-        for jp in range(4):
-            nc.vector.tensor_copy(out=patch_win[:, jp, :, :, :], in_=xp_by_four[:, :, :, 2 * jp : 2 * jp + IMG])
 
         cols_a = keep.tile([P, P], F32)
         cols_b = keep.tile([P, P], F32)

@@ -72,8 +72,6 @@ def tile_revolutionnaive_w_kernel(
         x2_first = KK // 4
         x3_first = x2_first + 2 * CH
         nc.vector.memset(feat_words[:, :, :, 0:x2_first], 0.0)
-        cm_rows = keep.tile([P, PCOLS], BF16)
-        nc.vector.memset(cm_rows[:].bitcast(F32), 0.0)
         w_planes = keep.tile([P, OUTS], U8, align_bytes=64)
         nc.vector.memset(w_planes[:].bitcast(I32), 0)
 
@@ -85,9 +83,13 @@ def tile_revolutionnaive_w_kernel(
         make_identity(nc, ident_f32[:])
         ident_bf16 = keep.tile([P, P], BF16)
         make_identity(nc, ident_bf16[:])
-        every_fourth = keep.tile([P, 768], BF16)
-        nc.gpsimd.memset(every_fourth[:], 0.0)
-        nc.gpsimd.tensor_copy(out=every_fourth[:, 268 : 268 + P], in_=ident_bf16[:])
+        pick_row = keep.tile([P, 4, P], BF16)
+        nc.gpsimd.memset(pick_row[:], 0.0)
+        ident_by_four = ident_bf16[:].rearrange("n (r a) -> n a r", a=4)
+        nc.gpsimd.tensor_copy(out=pick_row[:, :, PAD : PAD + IMG], in_=ident_by_four)
+        nc.gpsimd.tensor_copy(out=pick_row[:, :, 64 + PAD : 64 + PAD + IMG], in_=ident_by_four)
+        zero_cols = keep.tile([P, PROWS], BF16)
+        nc.gpsimd.memset(zero_cols[:], 0.0)
         two_blocks = keep.tile([P, 94, 2], BF16)
         nc.gpsimd.memset(two_blocks[:], 0.0)
         nc.gpsimd.tensor_copy(out=two_blocks[:, :, 0], in_=ident_bf16[:, 0:94])
@@ -119,10 +121,10 @@ def tile_revolutionnaive_w_kernel(
         grouped_words = grouped[:].bitcast(F32)
 
         xs_words = xs[:].bitcast(F32)
-        by_pixel = early_bank([P, 4, P])
+        by_pixel = psum.tile([P, 4, P], F32, tag="tp")
         for b in range(4):
             nc.tensor.transpose(by_pixel[:, b, :], xs_words[:, b : 4 * P : 4], ident_f32[:])
-        nc.scalar.copy(
+        nc.vector.tensor_copy(
             out=xp[:, PAD : PAD + IMG, PAD : PAD + IMG],
             in_=xs[:].rearrange("q (r s) -> q r s", s=IMG),
         )
@@ -134,34 +136,41 @@ def tile_revolutionnaive_w_kernel(
                 axis=AX.X,
                 op=ALU.max,
             )
-        row_image = early_bank([P, IMG])
+        row_image = psum.tile([P, PROWS], F32, tag="tp")
+        nc.tensor.matmul(out=row_image[:], lhsT=pick_row[:, 0, :], rhs=zero_cols[:], start=True, stop=True)
         for a in range(4):
-            for fh in range(2):
-                nc.tensor.matmul(
-                    out=row_image[:, 8 * a : 8 * (a + 1)],
-                    lhsT=every_fourth[:, a + 256 * (1 - fh) : a + 256 * (1 - fh) + 4 * (P - 1) + 1 : 4],
-                    rhs=pixel_max[:].rearrange("p b e -> p (b e)"),
-                    start=(fh == 0),
-                    stop=(fh == 1),
+            nc.tensor.matmul(
+                out=row_image[:, PAD + 8 * a : PAD + 8 * (a + 1)],
+                lhsT=pick_row[:, a, :],
+                rhs=pixel_max[:].rearrange("p b e -> p (b e)"),
+                start=True,
+                stop=True,
+            )
+        cm_wins = keep.tile([P, OHW // 2, 2, 4], BF16)
+        for fh in range(2):
+            for vpar in range(2):
+                first_col = 2 * vpar + 4 * fh
+                nc.scalar.copy(
+                    out=cm_wins[64 * fh : 64 * (fh + 1), :, vpar, :],
+                    in_=row_image[64 * fh : 64 * (fh + 1), first_col : first_col + IMG].rearrange(
+                        "k (w t) -> k w t", t=4
+                    ),
                 )
-        nc.scalar.copy(out=cm_rows[0:64, PAD : PAD + IMG], in_=row_image[0:64, :])
-        nc.scalar.copy(out=cm_rows[64:P, 0 : IMG - 1], in_=row_image[64:P, 1:IMG])
         x1_rows = keep.tile([P, 4 * POS], BF16)
         for h in range(HALVES):
-            x1_bank = early_bank([P, U2, OHW, 4])
+            x1_bank = psum.tile([P, U2, OHW * 4], F32, tag="tp")
             for u2 in range(U2):
                 shift = 2 * (4 * u2 + 2 * h)
-                for th in range(2):
-                    nc.tensor.matmul(
-                        out=x1_bank[:, u2, :, 2 * th : 2 * th + 2],
-                        lhsT=two_blocks_flat[:, shift : shift + P],
-                        rhs=cm_rows[:, 2 * th : 2 * th + 2 * OHW].rearrange("k (v two) -> k v two", two=2),
-                        start=True,
-                        stop=True,
-                    )
+                nc.tensor.matmul(
+                    out=x1_bank[:, u2, :],
+                    lhsT=two_blocks_flat[:, shift : shift + P],
+                    rhs=cm_wins[:].rearrange("k w vpar t -> k (w vpar t)"),
+                    start=True,
+                    stop=True,
+                )
             nc.scalar.copy(
                 out=x1_rows[0:x2_first, 4 * P * h : 4 * P * (h + 1)],
-                in_=x1_bank[0:x2_first].rearrange("k u2 v t -> k (u2 v t)"),
+                in_=x1_bank[0:x2_first].rearrange("k u2 c -> k (u2 c)"),
             )
 
         def flip_four(sources, bank):
@@ -180,7 +189,7 @@ def tile_revolutionnaive_w_kernel(
         patch_win = keep.tile([P, 4, 4, PROWS // 4, IMG], BF16)
         xp_by_four = xp[:].rearrange("q (a rho) s -> q rho a s", rho=4)
         for jp in range(4):
-            nc.vector.tensor_copy(out=patch_win[:, jp, :, :, :], in_=xp_by_four[:, :, :, 2 * jp : 2 * jp + IMG])
+            nc.scalar.copy(out=patch_win[:, jp, :, :, :], in_=xp_by_four[:, :, :, 2 * jp : 2 * jp + IMG])
 
         rows2 = keep.tile([P, HALF_ROWS, PCOLS], BF16)
         rows4 = keep.tile([P, HALF_ROWS - 1, PCOLS], BF16)
@@ -191,7 +200,7 @@ def tile_revolutionnaive_w_kernel(
         nc.vector.tensor_max(out=rows8[:], in0=rows4[:, 0:OHW, :], in1=rows4[:, 2 : OHW + 2, :])
         x2_win = keep.tile([P, 4, HALVES, U2, IMG], BF16)
         for jp in range(4):
-            nc.scalar.copy(
+            nc.vector.tensor_copy(
                 out=x2_win[:, jp, :, :, :].rearrange("q h u2 w -> q u2 h w"),
                 in_=rows8[:, :, 2 * jp : 2 * jp + IMG].rearrange("q (u2 h) w -> q u2 h w", h=HALVES),
             )

@@ -121,7 +121,7 @@ def tile_revolutionnaive_w_kernel(
         grouped_words = grouped[:].bitcast(F32)
 
         xs_words = xs[:].bitcast(F32)
-        by_pixel = psum.tile([P, 4, P], F32, tag="tp")
+        by_pixel = psum.tile([P, 4, P], F32, tag="mx")
         for b in range(4):
             nc.tensor.transpose(by_pixel[:, b, :], xs_words[:, b : 4 * P : 4], ident_f32[:])
         nc.vector.tensor_copy(
@@ -136,7 +136,7 @@ def tile_revolutionnaive_w_kernel(
                 axis=AX.X,
                 op=ALU.max,
             )
-        row_image = psum.tile([P, PROWS], F32, tag="tp")
+        row_image = psum.tile([P, PROWS], F32, tag="mx")
         nc.tensor.matmul(out=row_image[:], lhsT=pick_row[:, 0, :], rhs=zero_cols[:], start=True, stop=True)
         for a in range(4):
             nc.tensor.matmul(
@@ -157,21 +157,18 @@ def tile_revolutionnaive_w_kernel(
                     ),
                 )
         x1_rows = keep.tile([P, 4 * POS], BF16)
+        x1_bank = psum.tile([P, HALVES, U2, OHW * 4], BF16, tag="mx")
         for h in range(HALVES):
-            x1_bank = psum.tile([P, U2, OHW * 4], F32, tag="tp")
             for u2 in range(U2):
                 shift = 2 * (4 * u2 + 2 * h)
                 nc.tensor.matmul(
-                    out=x1_bank[:, u2, :],
+                    out=x1_bank[:, h, u2, :],
                     lhsT=two_blocks_flat[:, shift : shift + P],
                     rhs=cm_wins[:].rearrange("k w vpar t -> k (w vpar t)"),
                     start=True,
                     stop=True,
                 )
-            nc.scalar.copy(
-                out=x1_rows[0:x2_first, 4 * P * h : 4 * P * (h + 1)],
-                in_=x1_bank[0:x2_first].rearrange("k u2 c -> k (u2 c)"),
-            )
+        nc.scalar.copy(out=x1_rows[0:x2_first, :], in_=x1_bank[0:x2_first].rearrange("k h u2 c -> k (h u2 c)"))
 
         def flip_four(sources, bank):
             for f in range(4):
@@ -189,7 +186,7 @@ def tile_revolutionnaive_w_kernel(
         patch_win = keep.tile([P, 4, 4, PROWS // 4, IMG], BF16)
         xp_by_four = xp[:].rearrange("q (a rho) s -> q rho a s", rho=4)
         for jp in range(4):
-            nc.scalar.copy(out=patch_win[:, jp, :, :, :], in_=xp_by_four[:, :, :, 2 * jp : 2 * jp + IMG])
+            copy_on("vvss"[jp], patch_win[:, jp, :, :, :], xp_by_four[:, :, :, 2 * jp : 2 * jp + IMG])
 
         rows2 = keep.tile([P, HALF_ROWS, PCOLS], BF16)
         rows4 = keep.tile([P, HALF_ROWS - 1, PCOLS], BF16)

@@ -31,7 +31,8 @@ OUTS = CH * KK
 TILES = OUTS // P
 ROUND = 4
 BN_EPS = 1e-5
-W_BUFS = 12
+CHUNK_ROUNDS = 2
+W_BUFS = 6
 
 FLOPS = 2 * FEATS * OUTS * POS
 
@@ -276,14 +277,21 @@ def tile_revolutionnaive_w_kernel(
         w_words = conv_w_words.rearrange("g p n t -> p g (n t)")
         rounds = [(t0, min(ROUND, TILES - t0)) for t0 in range(0, TILES, ROUND)]
         z_of_round = {}
+        chunk_of_round = {}
 
         def multiply(r):
             t0, count = rounds[r]
-            chunk = weights.tile([P, PASSES, ROUND * P], I32, align_bytes=64)
-            nc.sync.dma_start(
-                out=chunk[:, :, 0 : count * P],
-                in_=w_words[:, :, 4 * P * t0 : 4 * P * (t0 + count)].bitcast(I32),
-            )
+            if r % CHUNK_ROUNDS == 0:
+                tiles_here = min(CHUNK_ROUNDS * ROUND, TILES - t0)
+                new_chunk = weights.tile([P, PASSES, CHUNK_ROUNDS * ROUND * P], I32, align_bytes=64)
+                nc.sync.dma_start(
+                    out=new_chunk[:, :, 0 : tiles_here * P],
+                    in_=w_words[:, :, 4 * P * t0 : 4 * P * (t0 + tiles_here)].bitcast(I32),
+                )
+                for later in range(CHUNK_ROUNDS):
+                    chunk_of_round[r + later] = new_chunk
+            chunk = chunk_of_round[r]
+            first_tile = ROUND * (r % CHUNK_ROUNDS)
             z_of_round[r] = []
             for a in range(count):
                 t = t0 + a
@@ -291,7 +299,7 @@ def tile_revolutionnaive_w_kernel(
                 for g in range(PASSES):
                     nc.tensor.matmul_mx(
                         out=acc[:],
-                        lhsT=chunk[:, g, P * a : P * (a + 1)].bitcast(FP8X4),
+                        lhsT=chunk[:, g, P * (first_tile + a) : P * (first_tile + a + 1)].bitcast(FP8X4),
                         lhsT_scale=w_planes[4 * g : P, P * t : P * (t + 1)],
                         rhs=f_codes[:, g, :].bitcast(FP8X4),
                         rhs_scale=f_planes[:, g, :],

@@ -52,10 +52,6 @@ def tile_revolutionnaive_w_kernel(
         rows_b = keep.tile([P, P], BF16)
         nc.vector.memset(rows_a[:].bitcast(F32), 0.0)
         nc.vector.memset(rows_b[:].bitcast(F32), 0.0)
-        nc.scalar.dma_start(out=rows_a[0:TILES, :], in_=bn_gamma.rearrange("(t p) -> t p", p=P))
-        nc.scalar.dma_start(out=rows_a[TILES : 2 * TILES, :], in_=bn_var.rearrange("(t p) -> t p", p=P))
-        nc.scalar.dma_start(out=rows_b[0:TILES, :], in_=bn_beta.rearrange("(t p) -> t p", p=P))
-        nc.scalar.dma_start(out=rows_b[TILES : 2 * TILES, :], in_=bn_mean.rearrange("(t p) -> t p", p=P))
 
         xs = keep.tile([P, IMG * IMG], BF16)
         nc.vector.memset(xs[0:LEAD, :].bitcast(F32), 0.0)
@@ -66,6 +62,10 @@ def tile_revolutionnaive_w_kernel(
                 out=xs[LEAD + first : LEAD + first + size, :], in_=x_rows[first : first + size, :]
             )
             first += size
+        nc.sync.dma_start(out=rows_a[0:TILES, :], in_=bn_gamma.rearrange("(t p) -> t p", p=P))
+        nc.sync.dma_start(out=rows_a[TILES : 2 * TILES, :], in_=bn_var.rearrange("(t p) -> t p", p=P))
+        nc.sync.dma_start(out=rows_b[0:TILES, :], in_=bn_beta.rearrange("(t p) -> t p", p=P))
+        nc.sync.dma_start(out=rows_b[TILES : 2 * TILES, :], in_=bn_mean.rearrange("(t p) -> t p", p=P))
         xp = keep.tile([P, PROWS, PCOLS], BF16)
         nc.vector.memset(xp[:].rearrange("q r s -> q (r s)").bitcast(F32), 0.0)
         feat_t = keep.tile([P, HALVES, 2, FEATS // 2], BF16)

import concourse.mybir as mybir
from concourse.masks import make_identity

F32 = mybir.dt.float32
BF16 = mybir.dt.bfloat16
I32 = mybir.dt.int32
U8 = mybir.dt.uint8
FP8X4 = mybir.dt.float8_e4m3fn_x4
ALU = mybir.AluOpType
ACT = mybir.ActivationFunctionType
AX = mybir.AxisListType

P = 128
CH = 124
LEAD = P - CH
IMG = 32
PAD = 3
PCOLS = IMG + 2 * PAD
PROWS = 40
WIN = 8
HALF_ROWS = 19
OHW = 16
POS = OHW * OHW
HALVES = 2
U2 = OHW // 2
WROWS = WIN + 2
KK = WIN * WIN
FEATS = 2 * WIN * CH + KK
PASSES = FEATS // (4 * P)
OUTS = CH * KK
TILES = OUTS // P
ROUND = 4
BN_EPS = 1e-5
CHUNK_ROUNDS = 2
W_BUFS = 6

FLOPS = 2 * FEATS * OUTS * POS


def tile_revolutionnaive_w_kernel(
    tc, x, conv_w_words, conv_w_scales, bn_gamma, bn_beta, bn_mean, bn_var, out
):
    nc = tc.nc
    with tc.tile_pool(name="keep", bufs=1) as keep, tc.tile_pool(
        name="weights", bufs=W_BUFS
    ) as weights, tc.tile_pool(name="zpool", bufs=3 * ROUND) as zpool, tc.tile_pool(
        name="prods", bufs=3
    ) as prods, tc.psum_pool(name="psum", bufs=4) as psum, tc.manual_schedule(
        engines={mybir.EngineType.SP}
    ):
        rows_a = keep.tile([P, P], BF16)
        rows_b = keep.tile([P, P], BF16)
        nc.vector.memset(rows_a[:].bitcast(F32), 0.0)
        nc.vector.memset(rows_b[:].bitcast(F32), 0.0)

        xs = keep.tile([P, IMG * IMG], BF16)
        nc.vector.memset(xs[0:LEAD, :].bitcast(F32), 0.0)
        x_rows = x.rearrange("b c r s -> (b c) (r s)")
        first = 0
        for size in (64, 32, 16, 8, 4):
            nc.sync.dma_start(
                out=xs[LEAD + first : LEAD + first + size, :], in_=x_rows[first : first + size, :]
            )
            first += size
        nc.sync.dma_start(out=rows_a[0:TILES, :], in_=bn_gamma.rearrange("(t p) -> t p", p=P))
        nc.sync.dma_start(out=rows_a[TILES : 2 * TILES, :], in_=bn_var.rearrange("(t p) -> t p", p=P))
        nc.sync.dma_start(out=rows_b[0:TILES, :], in_=bn_beta.rearrange("(t p) -> t p", p=P))
        nc.sync.dma_start(out=rows_b[TILES : 2 * TILES, :], in_=bn_mean.rearrange("(t p) -> t p", p=P))
        xp = keep.tile([P, PROWS, PCOLS], BF16)
        nc.vector.memset(xp[:].rearrange("q r s -> q (r s)").bitcast(F32), 0.0)
        feat_t = keep.tile([P, HALVES, 2, FEATS // 2], BF16)
        feat_words = feat_t[:].bitcast(F32)
        x2_first = KK // 4
        x3_first = x2_first + 2 * CH
        nc.vector.memset(feat_words[:, :, :, 0:x2_first], 0.0)
        w_planes = keep.tile([P, OUTS], U8, align_bytes=64)
        nc.vector.memset(w_planes[:].bitcast(I32), 0)

        warm = keep.tile([P, 1], F32)
        nc.gpsimd.memset(warm[:], 1.0)
        nc.scalar.activation(out=warm[:], in_=warm[:], func=ACT.Sqrt)

        ident_f32 = keep.tile([P, P], F32)
        make_identity(nc, ident_f32[:])
        ident_bf16 = keep.tile([P, P], BF16)
        make_identity(nc, ident_bf16[:])
        pick_row = keep.tile([P, 4, P], BF16)
        nc.gpsimd.memset(pick_row[:], 0.0)
        ident_by_four = ident_bf16[:].rearrange("n (r a) -> n a r", a=4)
        nc.gpsimd.tensor_copy(out=pick_row[:, :, PAD : PAD + IMG], in_=ident_by_four)
        nc.gpsimd.tensor_copy(out=pick_row[:, :, 64 + PAD : 64 + PAD + IMG], in_=ident_by_four)
        zero_cols = keep.tile([P, PROWS], BF16)
        nc.gpsimd.memset(zero_cols[:], 0.0)
        two_blocks = keep.tile([P, 94, 2], BF16)
        nc.gpsimd.memset(two_blocks[:], 0.0)
        nc.gpsimd.tensor_copy(out=two_blocks[:, :, 0], in_=ident_bf16[:, 0:94])
        nc.gpsimd.tensor_copy(out=two_blocks[:, 0:64, 1], in_=ident_bf16[:, 64:P])
        two_blocks_flat = two_blocks[:].rearrange("k c two -> k (c two)")

        for quad in range(4):
            nc.sync.dma_start(
                out=w_planes[32 * quad : 32 * quad + 16, :].bitcast(I32),
                in_=conv_w_scales[:, 4 * quad : 4 * quad + 4, :].bitcast(I32),
            )

        out_t = keep.tile([P, HALVES, P], F32)
        nc.gpsimd.memset(out_t[:], 0.0)

        def early_bank(shape):
            bank = psum.tile(shape, F32, tag="mx")
            return bank

        def copy_on(engine, dst, src):
            if engine == "v":
                nc.vector.tensor_copy(out=dst, in_=src)
            else:
                nc.scalar.copy(out=dst, in_=src)

        grouped = keep.tile([P, PASSES, 4 * POS], BF16, align_bytes=64)
        f_codes = keep.tile([P, PASSES, POS], I32, align_bytes=64)
        f_planes = keep.tile([P, PASSES, POS], U8, align_bytes=64)
        grouped_words = grouped[:].bitcast(F32)

        xs_words = xs[:].bitcast(F32)
        by_pixel = psum.tile([P, 4, P], F32, tag="mx")
        for b in range(4):
            nc.tensor.transpose(by_pixel[:, b, :], xs_words[:, b : 4 * P : 4], ident_f32[:])
        nc.vector.tensor_copy(
            out=xp[:, PAD : PAD + IMG, PAD : PAD + IMG],
            in_=xs[:].rearrange("q (r s) -> q r s", s=IMG),
        )
        pixel_max = keep.tile([P, 4, 2], BF16)
        with nc.allow_low_precision(reason="a maximum of bfloat16 values is a bfloat16 value"):
            nc.vector.tensor_reduce(
                out=pixel_max[:],
                in_=by_pixel[:].bitcast(BF16).rearrange("p b (q e) -> p b e q", e=2)[:, :, :, LEAD:P],
                axis=AX.X,
                op=ALU.max,
            )
        row_image = psum.tile([P, PROWS], F32, tag="mx")
        nc.tensor.matmul(out=row_image[:], lhsT=pick_row[:, 0, :], rhs=zero_cols[:], start=True, stop=True)
        for a in range(4):
            nc.tensor.matmul(
                out=row_image[:, PAD + 8 * a : PAD + 8 * (a + 1)],
                lhsT=pick_row[:, a, :],
                rhs=pixel_max[:].rearrange("p b e -> p (b e)"),
                start=True,
                stop=True,
            )
        cm_wins = keep.tile([P, OHW // 2, 2, 4], BF16)
        for fh in range(2):
            for vpar in range(2):
                first_col = 2 * vpar + 4 * fh
                nc.scalar.copy(
                    out=cm_wins[64 * fh : 64 * (fh + 1), :, vpar, :],
                    in_=row_image[64 * fh : 64 * (fh + 1), first_col : first_col + IMG].rearrange(
                        "k (w t) -> k w t", t=4
                    ),
                )
        x1_rows = keep.tile([P, 4 * POS], BF16)
        x1_bank = psum.tile([P, HALVES, U2, OHW * 4], BF16, tag="mx")
        for h in range(HALVES):
            for u2 in range(U2):
                shift = 2 * (4 * u2 + 2 * h)
                nc.tensor.matmul(
                    out=x1_bank[:, h, u2, :],
                    lhsT=two_blocks_flat[:, shift : shift + P],
                    rhs=cm_wins[:].rearrange("k w vpar t -> k (w vpar t)"),
                    start=True,
                    stop=True,
                )
        nc.scalar.copy(out=x1_rows[0:x2_first, :], in_=x1_bank[0:x2_first].rearrange("k h u2 c -> k (h u2 c)"))

        def flip_four(sources, bank):
            for f in range(4):
                nc.tensor.transpose(bank[:, f, :], sources[f], ident_f32[:])

        def flip_features(sources, h, first_n, engine):
            bank = early_bank([P, 4, P])
            flip_four(sources, bank)
            copy_on(
                engine,
                feat_words[:, h, :, first_n : first_n + 2 * CH].rearrange("p e (c fh) -> p e c fh", fh=2),
                bank[:, :, LEAD:P].rearrange("p (fh e) c -> p e c fh", e=2),
            )

        patch_win = keep.tile([P, 4, 4, PROWS // 4, IMG], BF16)
        xp_by_four = xp[:].rearrange("q (a rho) s -> q rho a s", rho=4)
        for jp in range(4):
            copy_on("vvss"[jp], patch_win[:, jp, :, :, :], xp_by_four[:, :, :, 2 * jp : 2 * jp + IMG])

        rows2 = keep.tile([P, HALF_ROWS, PCOLS], BF16)
        rows4 = keep.tile([P, HALF_ROWS - 1, PCOLS], BF16)
        rows8 = keep.tile([P, OHW, PCOLS], BF16)
        xp_row_pairs = xp[:, 0 : 2 * HALF_ROWS, :].rearrange("q (a two) s -> q a two s", two=2)
        nc.vector.tensor_max(out=rows2[:], in0=xp_row_pairs[:, :, 0, :], in1=xp_row_pairs[:, :, 1, :])
        nc.vector.tensor_max(out=rows4[:], in0=rows2[:, 0 : HALF_ROWS - 1, :], in1=rows2[:, 1:HALF_ROWS, :])
        nc.vector.tensor_max(out=rows8[:], in0=rows4[:, 0:OHW, :], in1=rows4[:, 2 : OHW + 2, :])
        x2_win = keep.tile([P, 4, HALVES, U2, IMG], BF16)
        for jp in range(4):
            nc.vector.tensor_copy(
                out=x2_win[:, jp, :, :, :].rearrange("q h u2 w -> q u2 h w"),
                in_=rows8[:, :, 2 * jp : 2 * jp + IMG].rearrange("q (u2 h) w -> q u2 h w", h=HALVES),
            )
        x2_words = x2_win[:].rearrange("q jp h u2 w -> q jp h (u2 w)").bitcast(F32)
        for h in range(HALVES):
            flip_features([x2_words[:, jp, h, :] for jp in range(4)], h, x2_first, "s")

        cols2 = keep.tile([P, PROWS, HALF_ROWS], BF16)
        cols4 = keep.tile([P, PROWS, HALF_ROWS - 1], BF16)
        xp_col_pairs = xp[:].rearrange("q r (b two) -> q r b two", two=2)
        nc.vector.tensor_max(out=cols2[:], in0=xp_col_pairs[:, :, :, 0], in1=xp_col_pairs[:, :, :, 1])
        nc.vector.tensor_max(out=cols4[:], in0=cols2[:, :, 0 : HALF_ROWS - 1], in1=cols2[:, :, 1:HALF_ROWS])
        x3_win = keep.tile([P, 2, PROWS // 4, OHW, 2], BF16)
        cols4_by_four = cols4[:].rearrange("q (a par e) b -> q par a b e", par=2, e=2)
        for par in range(2):
            nc.vector.tensor_max(
                out=x3_win[:, par, :, :, :],
                in0=cols4_by_four[:, par, :, 0:OHW, :],
                in1=cols4_by_four[:, par, :, 2 : OHW + 2, :],
            )
        x3_words = x3_win[:].rearrange("q par a v e -> q par (a v e)").bitcast(F32)
        for h in range(HALVES):
            flip_features(
                [
                    x3_words[:, (h + ip) % 2, OHW * ((h + ip) // 2) : OHW * ((h + ip) // 2) + P]
                    for ip in range(4)
                ],
                h,
                x3_first,
                "sv"[h],
            )

        cols_a = keep.tile([P, P], F32)
        cols_b = keep.tile([P, P], F32)
        for rows, cols in ((rows_a, cols_a), (rows_b, cols_b)):
            flipped = psum.tile([P, P], BF16, tag="mx")
            nc.tensor.transpose(flipped[:], rows[:], ident_bf16[:])
            nc.vector.tensor_copy(out=cols[:], in_=flipped[:])
        gamma, var = cols_a[:, 0:TILES], cols_a[:, TILES : 2 * TILES]
        beta, mean = cols_b[:, 0:TILES], cols_b[:, TILES : 2 * TILES]
        bn_scale = keep.tile([P, TILES], F32)
        bn_shift = keep.tile([P, TILES], F32)
        nc.scalar.activation(out=bn_scale[:], in_=var, func=ACT.Sqrt, bias=BN_EPS, scale=1.0)
        nc.vector.reciprocal(out=bn_scale[:], in_=bn_scale[:])
        nc.vector.tensor_mul(out=bn_scale[:], in0=bn_scale[:], in1=gamma)
        nc.vector.tensor_mul(out=bn_shift[:], in0=mean, in1=bn_scale[:])
        nc.vector.tensor_sub(out=bn_shift[:], in0=beta, in1=bn_shift[:])

        for g in (1, 0, 3, 2):
            bank = early_bank([P, 2, HALVES, P])
            for e in range(2):
                for h in range(HALVES):
                    nc.tensor.transpose(bank[:, e, h, :], feat_words[:, h, e, P * g : P * (g + 1)], ident_f32[:])
            copy_on(
                "ssvv"[g],
                grouped_words[:, g, :].rearrange("p (n e) -> p n e", e=2),
                bank[:].rearrange("p e h n -> p (h n) e"),
            )
            if g == 0:
                nc.vector.tensor_copy(out=grouped[0:x2_first, 0, :], in_=x1_rows[0:x2_first, :])
        for g in (1, 0, 3, 2):
            nc.vector.quantize_mx(
                out=f_codes[:, g, :].bitcast(FP8X4), scales=f_planes[:, g, :], in_=grouped[:, g, :]
            )

        patches = keep.tile([P, P, WROWS, WIN], BF16)
        patch_words = patches[:].bitcast(F32)
        win_words = patch_win[:].rearrange("q jp rho a w -> q jp rho (a w)").bitcast(F32)

        for r in range(WROWS):
            start = OHW * (r // 4)
            bank = psum.tile([P, 4, P], F32, tag="tp")
            flip_four([win_words[:, jp, r % 4, start : start + P] for jp in range(4)], bank)
            copy_on("ssssssvvvv"[r], patch_words[:, :, r, :], bank[:].rearrange("p f q -> p q f"))

        w_words = conv_w_words.rearrange("g p n t -> p g (n t)")
        rounds = [(t0, min(ROUND, TILES - t0)) for t0 in range(0, TILES, ROUND)]
        z_of_round = {}
        chunk_of_round = {}

        def multiply(r):
            t0, count = rounds[r]
            if r % CHUNK_ROUNDS == 0:
                tiles_here = min(CHUNK_ROUNDS * ROUND, TILES - t0)
                new_chunk = weights.tile([P, PASSES, CHUNK_ROUNDS * ROUND * P], I32, align_bytes=64)
                nc.sync.dma_start(
                    out=new_chunk[:, :, 0 : tiles_here * P],
                    in_=w_words[:, :, 4 * P * t0 : 4 * P * (t0 + tiles_here)].bitcast(I32),
                )
                for later in range(CHUNK_ROUNDS):
                    chunk_of_round[r + later] = new_chunk
            chunk = chunk_of_round[r]
            first_tile = ROUND * (r % CHUNK_ROUNDS)
            z_of_round[r] = []
            for a in range(count):
                t = t0 + a
                acc = psum.tile([P, POS], F32, tag="mx")
                for g in range(PASSES):
                    nc.tensor.matmul_mx(
                        out=acc[:],
                        lhsT=chunk[:, g, P * (first_tile + a) : P * (first_tile + a + 1)].bitcast(FP8X4),
                        lhsT_scale=w_planes[4 * g : P, P * t : P * (t + 1)],
                        rhs=f_codes[:, g, :].bitcast(FP8X4),
                        rhs_scale=f_planes[:, g, :],
                        start=(g == 0),
                        stop=(g == PASSES - 1),
                    )
                z = zpool.tile([P, POS], F32, tag="z")
                nc.scalar.activation(
                    out=z[:], in_=acc[:], func=ACT.Relu, bias=bn_shift[:, t : t + 1], scale=bn_scale[:, t : t + 1]
                )
                z_of_round[r].append(z)

        def apply_to_patches(r):
            t0, count = rounds[r]
            q0 = LEAD + 2 * t0
            for h in range(HALVES):
                z_t = psum.tile([P, ROUND * P], F32, tag="tp")
                for a in range(count):
                    nc.tensor.transpose(
                        z_t[:, P * a : P * (a + 1)], z_of_round[r][a][:, P * h : P * (h + 1)], ident_f32[:]
                    )
                prod = prods.tile([P, ROUND * P], F32, tag="prod")
                nc.vector.tensor_mul(
                    out=prod[:, 0 : count * P].rearrange("p (q k) -> p q k", k=KK),
                    in0=z_t[:, 0 : count * P].rearrange("p (q k) -> p q k", k=KK),
                    in1=patches[:, q0 : q0 + 2 * count, 2 * h : 2 * h + WIN, :].rearrange("p q i j -> p q (i j)"),
                )
                if h == 0:
                    nc.vector.tensor_reduce(
                        out=out_t[:, h, q0 : q0 + 2 * count],
                        in_=prod[:, 0 : count * P].rearrange("p (q k) -> p q k", k=KK),
                        axis=AX.X,
                        op=ALU.add,
                    )
                else:
                    for c in range(2 * count):
                        unused = prods.tile([P, KK], F32, tag="unused")
                        nc.scalar.activation(
                            out=unused[:],
                            in_=prod[:, KK * c : KK * (c + 1)],
                            func=ACT.Copy,
                            accum_out=out_t[:, h, q0 + c : q0 + c + 1],
                        )

        for r in range(len(rounds) + 1):
            if r < len(rounds):
                multiply(r)
            if r > 0:
                apply_to_patches(r - 1)

        by_channel = psum.tile([P, HALVES, P], F32, tag="tp")
        for h in range(HALVES):
            nc.tensor.transpose(by_channel[:, h, :], out_t[:, h, :], ident_f32[:])
        result = keep.tile([P, POS], F32)
        nc.vector.tensor_scalar_mul(
            out=result[:].rearrange("q (u2 h v) -> q h u2 v", h=HALVES, v=OHW),
            in0=by_channel[:].rearrange("q h (u2 v) -> q h u2 v", v=OHW),
            scalar1=1.0 / KK,
        )
        out_rows = out.rearrange("b c u v -> (b c) (u v)")
        first = 0
        for size in (64, 32, 16, 8, 4):
            nc.sync.dma_start(
                out=out_rows[first : first + size, :], in_=result[LEAD + first : LEAD + first + size, :]
            )
            first += size
